import numpy as np
import ml_dtypes


def mxq(x, axis, fmt="e4m3"):
    dtype, down = {"e4m3": (ml_dtypes.float8_e4m3fn, 7), "e5m2": (ml_dtypes.float8_e5m2, 14)}[fmt]
    v = np.moveaxis(np.asarray(x, np.float32).astype(ml_dtypes.bfloat16).astype(np.float64), axis, -1)
    blocks = v.reshape(v.shape[:-1] + (-1, 32))
    amax = np.abs(blocks).max(-1, keepdims=True)
    byte = np.maximum(np.where(amax > 0, np.frexp(amax)[1] - 1 + 127, 0) - down, 1)
    scale = np.exp2(byte - 127.0)
    codes = (blocks / scale).astype(np.float32).astype(dtype).astype(np.float64)
    return np.moveaxis((codes * scale).reshape(v.shape), -1, axis)


WIDE = False


def mx_kscale(k):
    if not WIDE:
        return np.ones(k)
    levels = np.array([10, -10, 5, -5, 0])
    if k % 512:
        return np.exp2(np.random.permutation(np.resize(levels, k // 32))).repeat(32)
    a = np.empty((k // 512, 16))
    for p in range(k // 512):
        a[p, :8] = np.random.permutation(np.resize(levels, 8))
        for g in range(8):
            far = levels[np.abs(levels - a[p, g]) >= 10]
            a[p, g + 8] = far[np.random.randint(len(far))]
    return np.exp2(a.ravel()).repeat(32)


BF16 = ml_dtypes.bfloat16


def bf(x):
    return np.asarray(x, np.float32).astype(BF16)


def f64(x):
    return np.asarray(x).astype(np.float64)


B, E, P, H, HK, D = 16, 256, 768, 4, 2, 128
G = H // HK
S = P + E
SCALING = 1.0 / np.sqrt(D)


def setup_inputs():
    s = mx_kscale(S)
    a = np.log2(s)
    g = s.max() / s
    q = np.random.standard_normal((B, E, H, D)) * 2.0
    k = np.random.standard_normal((B, E, HK, D))
    v = np.random.standard_normal((B, E, HK, D)) * 2.0
    k_cache = np.random.standard_normal((B, P, HK, D))
    v_cache = np.random.standard_normal((B, P, HK, D)) * 2.0
    q[..., 0] = np.log(2.0) * np.sqrt(D)
    k_cache[..., 0] += a[:P][None, :, None]
    k[..., 0] += a[P:][None, :, None]
    v_cache *= g[:P][None, :, None, None]
    v *= g[P:][None, :, None, None]
    return {"q": bf(q), "k": bf(k), "v": bf(v), "k_cache": bf(k_cache), "v_cache": bf(v_cache)}


def reference(q, k, v, k_cache, v_cache):
    k_all = np.concatenate([f64(k_cache), f64(k)], axis=1)
    v_all = np.concatenate([f64(v_cache), f64(v)], axis=1)
    qg = f64(q).reshape(B, E, HK, G, D).transpose(0, 2, 3, 1, 4).reshape(B, HK, G * E, D)
    scores = ((qg @ k_all.transpose(0, 2, 3, 1)) * SCALING).reshape(B, HK, G, E, S)
    visible = np.arange(S)[None, :] <= (P + np.arange(E))[:, None]
    scores = np.where(visible[None, None, None, :, :], scores, -1e30)
    e = np.exp(scores - scores.max(-1, keepdims=True))
    o = mxq(e, 4, "e4m3").reshape(B, HK, G * E, S) @ mxq(v_all, 1, "e4m3").transpose(0, 2, 1, 3)
    o = o.reshape(B, HK, G, E, D) / e.sum(-1, keepdims=True)
    return o.transpose(0, 3, 1, 2, 4).reshape(B * E, H * D)

@@ -1,0 +1,367 @@
+from contextlib import ExitStack
+import math
+
+import concourse.mybir as mybir
+from concourse.masks import make_identity
+
+FP8X4 = mybir.dt.float8_e4m3fn_x4
+BF16 = mybir.dt.bfloat16
+F32 = mybir.dt.float32
+U32 = mybir.dt.uint32
+U8 = mybir.dt.uint8
+ALU = mybir.AluOpType
+ACTF = mybir.ActivationFunctionType
+
+B, E, PRE, H, HK, D = 16, 256, 768, 4, 2, 128
+S = PRE + E
+P = 128
+SCALING = 1.0 / math.sqrt(D)
+NEG = -1.0e30
+FLOPS = 2 * 2 * B * H * E * S * D
+
+NU = B * 8
+HALF = S // 2
+DIAG = 64
+
+
+def tile_radixattention_t_kernel(tc, q, k, v, k_cache, v_cache, out):
+    nc = tc.nc
+    with ExitStack() as ctx:
+        ctx.enter_context(tc.manual_schedule())
+        const = ctx.enter_context(tc.tile_pool(name="const", bufs=1))
+        raw = ctx.enter_context(tc.tile_pool(name="raw", bufs=4))
+        prep = ctx.enter_context(tc.tile_pool(name="prep", bufs=2))
+        work = ctx.enter_context(tc.tile_pool(name="work", bufs=4))
+        two_buf = ctx.enter_context(tc.tile_pool(name="two_buf", bufs=2))
+        small = ctx.enter_context(tc.tile_pool(name="small", bufs=6))
+        ps_s = ctx.enter_context(tc.psum_pool(name="ps_s", bufs=4))
+        ps_t = ctx.enter_context(tc.psum_pool(name="ps_t", bufs=2))
+        ps_p = ctx.enter_context(tc.psum_pool(name="ps_p", bufs=1))
+        ps_o = ctx.enter_context(tc.psum_pool(name="ps_o", bufs=1))
+
+        q_v = q.rearrange("b (qb p) h d -> b p qb (h d)", p=P)
+        k_v = k.rearrange("b (c p) hk d -> b p c (hk d)", p=P)
+        kc_v = k_cache.rearrange("b (c p) hk d -> b p c (hk d)", p=P)
+        v_v = v.rearrange("b (p t) hk d -> b p t (hk d)", t=4)
+        vc_v = v_cache.rearrange("b (gp t) hk d -> b gp t (hk d)", t=4)
+
+        kraw_t, qraw_t, vraw_t = {}, {}, {}
+        kt_t, qt_t, vg_t, vcod_t, vsc_t = {}, {}, {}, {}, {}
+
+        def load(b):
+            qraw = raw.tile([P, 2, H * D], BF16, tag="qraw")
+            nc.sync.dma_start(out=qraw[:], in_=q_v[b])
+            kraw = raw.tile([P, 8, HK * D], BF16, tag="kraw")
+            nc.sync.dma_start(out=kraw[:, 0:6, :], in_=kc_v[b])
+            nc.sync.dma_start(out=kraw[:, 6:8, :], in_=k_v[b])
+            vraw = raw.tile([P, 2, 4, HK * D], BF16, tag="vraw")
+            nc.sync.dma_start(out=vraw[:, 0, :, :], in_=vc_v[b, 0:P])
+            nc.sync.dma_start(out=vraw[0:64, 1, :, :], in_=vc_v[b, P : P + 64])
+            nc.sync.dma_start(out=vraw[64:P, 1, :, :], in_=v_v[b])
+            kraw_t[b], qraw_t[b], vraw_t[b] = kraw, qraw, vraw
+
+        for b in range(3):
+            load(b)
+
+        ident = const.tile([P, P], BF16, name="ident")
+        make_identity(nc, ident[:])
+        ident32 = const.tile([P, P], F32, name="ident32")
+        make_identity(nc, ident32[:])
+        mask32 = const.tile([P, P], F32, name="mask32")
+        nc.gpsimd.memset(mask32[:], 0.0)
+        nc.gpsimd.affine_select(
+            out=mask32[:],
+            in_=mask32[:],
+            compare_op=ALU.is_ge,
+            fill=NEG,
+            base=0,
+            pattern=[[-1, P]],
+            channel_multiplier=1,
+        )
+        mask = const.tile([P, 2, DIAG], BF16, name="mask")
+        nc.vector.tensor_copy(
+            out=mask[:].rearrange("p u (z e) -> p u z e", e=2),
+            in_=mask32[:].rearrange("p (z u e) -> p u z e", u=2, e=2),
+        )
+        ezs = []
+        for i in range(4):
+            ez = const.tile([P, S], BF16, name="ez%d" % i)
+            nc.vector.memset(ez[:, HALF - DIAG : HALF], 0.0)
+            nc.vector.memset(ez[:, S - DIAG : S], 0.0)
+            ezs.append(ez)
+        warm = const.tile([P, 1], F32, name="warm")
+        nc.vector.memset(warm[:], 0.0)
+        warm2 = const.tile([P, 1], F32, name="warm2")
+        nc.scalar.activation(out=warm2[:], in_=warm[:], func=ACTF.Exp)
+
+        def copy_out(on_vector, dst, src):
+            if on_vector:
+                nc.vector.tensor_copy(out=dst, in_=src)
+            else:
+                nc.scalar.copy(out=dst, in_=src)
+
+        def prep_k(b, hk, on_vector, pool=ps_p, tag="p"):
+            if hk == 0:
+                kt = prep.tile([P, HK, S], BF16, tag="kt")
+                kt_t[b] = kt
+            tp = pool.tile([P, S], BF16, tag=tag)
+
+            def one(c):
+                return lambda: nc.tensor.transpose(
+                    out=tp[:, c * P : (c + 1) * P],
+                    in_=kraw_t[b][:, c, hk * D : (hk + 1) * D],
+                    identity=ident[:],
+                )
+
+            return [one(c) for c in range(8)], lambda: copy_out(
+                on_vector,
+                kt_t[b][:, hk, :].bitcast(F32).rearrange("p (u x) -> p u x", u=2),
+                tp[:].bitcast(F32).rearrange("p (x u) -> p u x", u=2),
+            )
+
+        def prep_q(b, on_vector, pool=ps_p, tag="p"):
+            qt = prep.tile([P, 8 * P], BF16, tag="qt")
+            qt_t[b] = qt
+            tp = pool.tile([P, S], BF16, tag=tag)
+
+            def one(i):
+                return lambda: nc.tensor.transpose(
+                    out=tp[:, i * P : (i + 1) * P],
+                    in_=qraw_t[b][:, i // 4, (i % 4) * D : (i % 4 + 1) * D],
+                    identity=ident[:],
+                )
+
+            return [one(i) for i in range(8)], lambda: copy_out(
+                on_vector, qt[:].bitcast(F32), tp[:].bitcast(F32)
+            )
+
+        def prep_v_copy(b, g):
+            if g == 0:
+                vg = prep.tile([P, 2, HK * D, 4], BF16, tag="vg", align_bytes=64)
+                vg_t[b] = vg
+            nc.vector.tensor_copy(
+                out=vg_t[b][:, g, :, :].rearrange("p (c i) t -> p c t i", i=4),
+                in_=vraw_t[b][:, g, :, :].rearrange("p t (c i) -> p c t i", i=4),
+            )
+
+        def prep_v_quantize(b):
+            vcod = prep.tile([P, 2 * HK * D], U32, tag="vcod", align_bytes=64)
+            vsc = prep.tile([P, 2 * HK * D], U8, tag="vsc", align_bytes=64)
+            vcod_t[b], vsc_t[b] = vcod, vsc
+            nc.vector.quantize_mx(
+                out=vcod[:].bitcast(FP8X4),
+                scales=vsc[:],
+                in_=vg_t[b][:].rearrange("p g x t -> p (g x t)"),
+            )
+
+        st = {}
+        gr = {}
+
+        def unit(u):
+            return u // 8, (u % 8) // 4, u % 4
+
+        def width(u):
+            return HALF - DIAG if unit(u)[1] == 0 else HALF
+
+        def stage_s(u, half):
+            b, qb, h = unit(u)
+            s = ps_s.tile([P, HALF], F32, tag="s")
+            w = width(u)
+            lhsT = qt_t[b][:, (qb * 4 + h) * P : (qb * 4 + h + 1) * P]
+            c0 = half * HALF
+            nc.tensor.matmul(
+                out=s[:, 0 : w - DIAG],
+                lhsT=lhsT,
+                rhs=kt_t[b][:, h // 2, c0 : c0 + w - DIAG],
+                start=True,
+                stop=True,
+            )
+            nc.tensor.matmul(
+                out=s[:, w - DIAG : w],
+                lhsT=lhsT,
+                rhs=kt_t[b][:, h // 2, c0 + w - DIAG : c0 + w],
+                start=True,
+                stop=False,
+            )
+            nc.tensor.matmul(
+                out=s[:, w - DIAG : w], lhsT=ident[:], rhs=mask[:, half, :], start=False, stop=True
+            )
+            st.setdefault(u, {})[half] = s
+
+        def stage_m(u, half):
+            d = st[u]
+            w = width(u)
+            if half == 0:
+                ssb = work.tile([P, S], F32, tag="ssb")
+                d["ssb"] = ssb
+            m = small.tile([P, 1], F32, tag="m%d" % half)
+            nc.vector.tensor_scalar(
+                out=d["ssb"][:, half * HALF : half * HALF + w],
+                in0=d[half][:, 0:w],
+                scalar1=-SCALING,
+                scalar2=None if half == 0 else d["m"][:, 0:1],
+                op0=ALU.mult,
+                op1=ALU.min,
+                accum_out=m[:],
+            )
+            d["m"] = m
+
+        def stage_e(u):
+            b, qb, h = unit(u)
+            d = st[u]
+            if h == 0:
+                ssum = small.tile([P, 4], F32, tag="ssum")
+                gr[u // 4] = {"ssum": ssum}
+            if qb == 0:
+                e = ezs[h]
+            else:
+                e = work.tile([P, S], BF16, tag="e")
+            w = width(u)
+            nc.scalar.activation(
+                out=e[:].rearrange("p (u x) -> p u x", u=2)[:, :, 0:w],
+                in_=d["ssb"][:].rearrange("p (u x) -> p u x", u=2)[:, :, 0:w],
+                func=ACTF.Exp,
+                bias=d["m"][:],
+                scale=-1.0,
+                accum_out=gr[u // 4]["ssum"][:, h : h + 1],
+            )
+            d["e"] = e
+
+        def stage_t(u):
+            d = st[u]
+            tp = ps_t.tile([P, 2, 2, P], F32, tag="t")
+            d["tp"] = tp
+            words = d["e"][:].bitcast(F32)
+
+            def one(g, half):
+                w0 = half * (HALF // 2) + g * P
+                return lambda: nc.tensor.transpose(
+                    out=tp[:, g, half, :], in_=words[:, w0 : w0 + P], identity=ident32[:]
+                )
+
+            return [one(g, half) for g in range(2) for half in range(2)]
+
+        def stage_c(u):
+            d = st[u]
+            gq = work.tile([P, S], BF16, tag="gq", align_bytes=64)
+            d["gq"] = gq
+            nc.scalar.copy(
+                out=gq[:].bitcast(F32).rearrange("p (g r u) -> p g r u", g=2, u=2),
+                in_=d["tp"][:].rearrange("p g u r -> p g r u"),
+            )
+
+        def stage_q(u):
+            d = gr[u // 4]
+            h = u % 4
+            if h == 0:
+                ecod = two_buf.tile([P, 8 * P], U32, tag="ecod", align_bytes=64)
+                esc = two_buf.tile([P, 8 * P], U8, tag="esc", align_bytes=64)
+                d["ecod"], d["esc"] = ecod, esc
+            cols = slice(h * 2 * P, (h + 1) * 2 * P)
+            nc.vector.quantize_mx(
+                out=d["ecod"][:, cols].bitcast(FP8X4), scales=d["esc"][:, cols], in_=st[u]["gq"][:]
+            )
+
+        def stage_x(su):
+            b = su // 2
+            d = gr[su]
+            o_ps = ps_o.tile([P, H * D], F32, tag="o")
+            d["o_ps"] = o_ps
+            for h in range(H):
+                for g in range(2):
+                    vcols = slice((g * HK + h // 2) * D, (g * HK + h // 2 + 1) * D)
+                    ecols = slice((h * 2 + g) * P, (h * 2 + g + 1) * P)
+                    nc.tensor.matmul_mx(
+                        out=o_ps[:, h * D : (h + 1) * D],
+                        lhsT=d["ecod"][:, ecols].bitcast(FP8X4),
+                        lhsT_scale=d["esc"][:, ecols],
+                        rhs=vcod_t[b][:, vcols].bitcast(FP8X4),
+                        rhs_scale=vsc_t[b][:, vcols],
+                        start=(g == 0),
+                        stop=(g == 1),
+                    )
+
+        def stage_r(su):
+            rinv = small.tile([P, 4], F32, tag="rinv")
+            nc.vector.reciprocal(out=rinv[:], in_=gr[su]["ssum"][:])
+            gr[su]["rinv"] = rinv
+
+        def stage_n(su):
+            b, qb = su // 2, su % 2
+            o_sb = work.tile([P, H, D], F32, tag="o_sb")
+            nc.vector.tensor_tensor(
+                out=o_sb[:],
+                in0=gr[su]["o_ps"][:].rearrange("p (h d) -> p h d", h=H),
+                in1=gr[su]["rinv"][:].unsqueeze(2).to_broadcast([P, H, D]),
+                op=ALU.mult,
+            )
+            r0 = b * E + qb * P
+            nc.sync.dma_start(out=out[r0 : r0 + P, :], in_=o_sb[:].rearrange("p h d -> p (h d)"))
+
+        def run(calls):
+            for call in calls:
+                call()
+
+        def ok(u):
+            return 0 <= u < NU
+
+        first = prep_q(0, False, ps_t, "t")
+        run(first[0])
+        first[1]()
+        first = prep_k(0, 0, True, ps_t, "t")
+        run(first[0])
+        first[1]()
+        group = prep_k(0, 1, False)
+        waiting = group[0]
+
+        for step in range(-3, NU + 9):
+            nxt = step // 8 + 1
+            i = step % 8
+            prepare = 0 <= step < NU and nxt < B
+            if ok(step - 1):
+                stage_e(step - 1)
+            if ok(step + 2):
+                stage_m(step + 2, 0)
+            if ok(step - 8) and (step - 8) % 4 == 0:
+                stage_n((step - 8) // 4)
+            if ok(step + 1):
+                stage_m(step + 1, 1)
+            tr = []
+            if ok(step - 2):
+                tr = stage_t(step - 2)
+            if prepare and i in (0, 2, 4):
+                if i == 0:
+                    group = prep_k(nxt, 0, False)
+                elif i == 2:
+                    group = prep_q(nxt, False)
+                else:
+                    group = prep_k(nxt, 1, False)
+                waiting = group[0]
+            late = 0 < len(waiting) <= 4
+            tr = tr + waiting[0:4]
+            waiting = waiting[4:]
+            if ok(step + 3):
+                stage_s(step + 3, 0)
+            run(tr)
+            if ok(step + 2):
+                stage_s(step + 2, 1)
+            if ok(step - 7) and (step - 7) % 4 == 0:
+                stage_x((step - 7) // 4)
+            if ok(step - 3):
+                stage_q(step - 3)
+            if ok(step - 2):
+                stage_c(step - 2)
+            if step in (0, 1):
+                prep_v_copy(0, step)
+            if step == 2:
+                prep_v_quantize(0)
+            if prepare and i in (3, 5):
+                prep_v_copy(nxt, (i - 3) // 2)
+            if prepare and i == 7:
+                prep_v_quantize(nxt)
+            if ok(step - 6) and (step - 6) % 4 == 0:
+                stage_r((step - 6) // 4)
+            if late:
+                group[1]()
+            if prepare and i == 0 and nxt + 2 < B:
+                load(nxt + 2)

@@ -135,13 +135,18 @@ def tile_radixattention_t_kernel(tc, q, k, v, k_cache, v_cache, out):
                 on_vector, qt[:].bitcast(F32), tp[:].bitcast(F32)
             )
 
-        def prep_v_copy(b, g):
-            if g == 0:
+        def prep_v_copy(b, piece):
+            if piece == 0:
                 vg = prep.tile([P, 2, HK * D, 4], BF16, tag="vg", align_bytes=64)
                 vg_t[b] = vg
-            nc.vector.tensor_copy(
-                out=vg_t[b][:, g, :, :].rearrange("p (c i) t -> p c t i", i=4),
-                in_=vraw_t[b][:, g, :, :].rearrange("p t (c i) -> p c t i", i=4),
+            g, hk = divmod(piece, 2)
+            nc.gpsimd.tensor_scalar(
+                out=vg_t[b][:, g, hk * D : (hk + 1) * D, :],
+                in0=vraw_t[b][:, g, :, hk * D : (hk + 1) * D].rearrange("p t x -> p x t"),
+                scalar1=1.0,
+                scalar2=0.0,
+                op0=ALU.mult,
+                op1=ALU.add,
             )
 
         def prep_v_quantize(b):
@@ -351,12 +356,12 @@ def tile_radixattention_t_kernel(tc, q, k, v, k_cache, v_cache, out):
                 stage_q(step - 3)
             if ok(step - 2):
                 stage_c(step - 2)
-            if step in (0, 1):
+            if step in (0, 1, 2, 3):
                 prep_v_copy(0, step)
-            if step == 2:
+            if step == 4:
                 prep_v_quantize(0)
-            if prepare and i in (3, 5):
-                prep_v_copy(nxt, (i - 3) // 2)
+            if prepare and 2 <= i < 6:
+                prep_v_copy(nxt, i - 2)
             if prepare and i == 7:
                 prep_v_quantize(nxt)
             if ok(step - 6) and (step - 6) % 4 == 0:

@@ -83,6 +83,11 @@ def tile_radixattention_t_kernel(tc, q, k, v, k_cache, v_cache, out):
             out=mask[:].rearrange("p u (z e) -> p u z e", e=2),
             in_=mask32[:].rearrange("p (z u e) -> p u z e", u=2, e=2),
         )
+        sums = []
+        for i in range(6):
+            ssum = const.tile([P, 5], F32, name="ssum%d" % i)
+            nc.vector.memset(ssum[:, 4:5], 1.0)
+            sums.append(ssum)
         ezs = []
         for i in range(4):
             ez = const.tile([P, S], BF16, name="ez%d" % i)
@@ -135,15 +140,14 @@ def tile_radixattention_t_kernel(tc, q, k, v, k_cache, v_cache, out):
                 on_vector, qt[:].bitcast(F32), tp[:].bitcast(F32)
             )
 
-        def prep_v_copy(b, piece):
-            if piece == 0:
+        def prep_v_copy(b, g, one):
+            if g == 0:
                 vg = prep.tile([P, 2, HK * D, 4], BF16, tag="vg", align_bytes=64)
                 vg_t[b] = vg
-            g, hk = divmod(piece, 2)
             nc.gpsimd.tensor_scalar(
-                out=vg_t[b][:, g, hk * D : (hk + 1) * D, :],
-                in0=vraw_t[b][:, g, :, hk * D : (hk + 1) * D].rearrange("p t x -> p x t"),
-                scalar1=1.0,
+                out=vg_t[b][:, g, :, :],
+                in0=vraw_t[b][:, g, :, :].rearrange("p t x -> p x t"),
+                scalar1=one,
                 scalar2=0.0,
                 op0=ALU.mult,
                 op1=ALU.add,
@@ -215,8 +219,7 @@ def tile_radixattention_t_kernel(tc, q, k, v, k_cache, v_cache, out):
             b, qb, h = unit(u)
             d = st[u]
             if h == 0:
-                ssum = small.tile([P, 4], F32, tag="ssum")
-                gr[u // 4] = {"ssum": ssum}
+                gr[u // 4] = {"ssum": sums[(u // 4) % 6]}
             if qb == 0:
                 e = ezs[h]
             else:
@@ -287,7 +290,7 @@ def tile_radixattention_t_kernel(tc, q, k, v, k_cache, v_cache, out):
                     )
 
         def stage_r(su):
-            rinv = small.tile([P, 4], F32, tag="rinv")
+            rinv = small.tile([P, 5], F32, tag="rinv")
             nc.vector.reciprocal(out=rinv[:], in_=gr[su]["ssum"][:])
             gr[su]["rinv"] = rinv
 
@@ -297,7 +300,7 @@ def tile_radixattention_t_kernel(tc, q, k, v, k_cache, v_cache, out):
             nc.vector.tensor_tensor(
                 out=o_sb[:],
                 in0=gr[su]["o_ps"][:].rearrange("p (h d) -> p h d", h=H),
-                in1=gr[su]["rinv"][:].unsqueeze(2).to_broadcast([P, H, D]),
+                in1=gr[su]["rinv"][:, 0:4].unsqueeze(2).to_broadcast([P, H, D]),
                 op=ALU.mult,
             )
             r0 = b * E + qb * P
@@ -356,16 +359,19 @@ def tile_radixattention_t_kernel(tc, q, k, v, k_cache, v_cache, out):
                 stage_q(step - 3)
             if ok(step - 2):
                 stage_c(step - 2)
-            if step in (0, 1, 2, 3):
-                prep_v_copy(0, step)
-            if step == 4:
-                prep_v_quantize(0)
-            if prepare and 2 <= i < 6:
-                prep_v_copy(nxt, i - 2)
-            if prepare and i == 7:
-                prep_v_quantize(nxt)
-            if ok(step - 6) and (step - 6) % 4 == 0:
-                stage_r((step - 6) // 4)
+            if step in (-3, -2):
+                prep_v_copy(0, step + 3, 1.0)
+            if 0 <= step < NU and i == 5:
+                prep_v_quantize(step // 8)
+            if ok(step - 7) and (step - 7) % 4 == 0:
+                su = (step - 7) // 4
+                stage_r(su)
+                if step < NU:
+                    one = gr[su]["rinv"][:, 4:5]
+                    if i == 7 and step // 8 + 1 < B:
+                        prep_v_copy(step // 8 + 1, 0, one)
+                    if i == 3 and step >= 8:
+                        prep_v_copy(step // 8, 1, one)
             if late:
                 group[1]()
             if prepare and i == 0 and nxt + 2 < B:

@@ -251,10 +251,13 @@ def tile_radixattention_t_kernel(tc, q, k, v, k_cache, v_cache, out):
 
         def stage_c(u):
             d = st[u]
-            gq = work.tile([P, S], BF16, tag="gq", align_bytes=64)
-            d["gq"] = gq
+            if u % 2 == 0:
+                gq = work.tile([P, 2, S], BF16, tag="gq", align_bytes=64)
+                gr[u // 4]["gq%d" % (u % 4)] = gq
+            else:
+                gq = gr[u // 4]["gq%d" % (u % 4 - 1)]
             nc.scalar.copy(
-                out=gq[:].bitcast(F32).rearrange("p (g r u) -> p g r u", g=2, u=2),
+                out=gq[:, u % 2, :].bitcast(F32).rearrange("p (g r u) -> p g r u", g=2, u=2),
                 in_=d["tp"][:].rearrange("p g u r -> p g r u"),
             )
 
@@ -265,9 +268,11 @@ def tile_radixattention_t_kernel(tc, q, k, v, k_cache, v_cache, out):
                 ecod = two_buf.tile([P, 8 * P], U32, tag="ecod", align_bytes=64)
                 esc = two_buf.tile([P, 8 * P], U8, tag="esc", align_bytes=64)
                 d["ecod"], d["esc"] = ecod, esc
-            cols = slice(h * 2 * P, (h + 1) * 2 * P)
+            cols = slice(h * 2 * P, (h + 2) * 2 * P)
             nc.vector.quantize_mx(
-                out=d["ecod"][:, cols].bitcast(FP8X4), scales=d["esc"][:, cols], in_=st[u]["gq"][:]
+                out=d["ecod"][:, cols].bitcast(FP8X4),
+                scales=d["esc"][:, cols],
+                in_=d["gq%d" % h][:].rearrange("p u x -> p (u x)"),
             )
 
         def stage_x(su):
@@ -355,8 +360,8 @@ def tile_radixattention_t_kernel(tc, q, k, v, k_cache, v_cache, out):
                 stage_s(step + 2, 1)
             if ok(step - 7) and (step - 7) % 4 == 0:
                 stage_x((step - 7) // 4)
-            if ok(step - 3):
-                stage_q(step - 3)
+            if ok(step - 4) and step % 2 == 0:
+                stage_q(step - 4)
             if ok(step - 2):
                 stage_c(step - 2)
             if step in (-3, -2):

@@ -344,7 +344,7 @@ def tile_radixattention_t_kernel(tc, q, k, v, k_cache, v_cache, out):
                 tr = stage_t(step - 2)
             if prepare and i in (0, 2, 4):
                 if i == 0:
-                    group = prep_k(nxt, 0, False)
+                    group = prep_k(nxt, 0, True)
                 elif i == 2:
                     group = prep_q(nxt, False)
                 else:

@@ -19,9 +19,12 @@ SCALING = 1.0 / math.sqrt(D)
 NEG = -1.0e30
 FLOPS = 2 * 2 * B * H * E * S * D
 
-NU = B * 8
+G = H // HK
+NJ = 4
+R = E // NJ
+NU = B * HK * NJ
 HALF = S // 2
-DIAG = 64
+DIAG = R // 2
 
 
 def tile_radixattention_t_kernel(tc, q, k, v, k_cache, v_cache, out):
@@ -42,6 +45,7 @@ def tile_radixattention_t_kernel(tc, q, k, v, k_cache, v_cache, out):
         q_v = q.rearrange("b (qb p) h d -> b p qb (h d)", p=P)
         k_v = k.rearrange("b (c p) hk d -> b p c (hk d)", p=P)
         kc_v = k_cache.rearrange("b (c p) hk d -> b p c (hk d)", p=P)
+        out_v = out.rearrange("(b j r) (hk hh d) -> b hk hh r j d", j=NJ, r=R, hk=HK, hh=G)
         v_v = v.rearrange("b (p t) hk d -> b p t (hk d)", t=4)
         vc_v = v_cache.rearrange("b (gp t) hk d -> b gp t (hk d)", t=4)
 
@@ -67,21 +71,27 @@ def tile_radixattention_t_kernel(tc, q, k, v, k_cache, v_cache, out):
         make_identity(nc, ident[:])
         ident32 = const.tile([P, P], F32, name="ident32")
         make_identity(nc, ident32[:])
-        mask32 = const.tile([P, P], F32, name="mask32")
-        nc.gpsimd.memset(mask32[:], 0.0)
-        nc.gpsimd.affine_select(
-            out=mask32[:],
-            in_=mask32[:],
-            compare_op=ALU.is_ge,
-            fill=NEG,
-            base=0,
-            pattern=[[-1, P]],
-            channel_multiplier=1,
-        )
+        mask_h = []
+        for hh in range(G):
+            mh = const.tile([P, R], F32, name="mask_h%d" % hh)
+            nc.gpsimd.memset(mh[:], 0.0)
+            nc.gpsimd.affine_select(
+                out=mh[:],
+                in_=mh[:],
+                compare_op=ALU.is_ge,
+                fill=NEG,
+                base=-hh * R,
+                pattern=[[-1, R]],
+                channel_multiplier=1,
+            )
+            mask_h.append(mh)
+        nc.gpsimd.memset(mask_h[1][0:R, :], 0.0)
         mask = const.tile([P, 2, DIAG], BF16, name="mask")
-        nc.vector.tensor_copy(
+        nc.vector.tensor_tensor(
             out=mask[:].rearrange("p u (z e) -> p u z e", e=2),
-            in_=mask32[:].rearrange("p (z u e) -> p u z e", u=2, e=2),
+            in0=mask_h[0][:].rearrange("p (z u e) -> p u z e", u=2, e=2),
+            in1=mask_h[1][:].rearrange("p (z u e) -> p u z e", u=2, e=2),
+            op=ALU.add,
         )
         sums = []
         for i in range(6):
@@ -89,10 +99,11 @@ def tile_radixattention_t_kernel(tc, q, k, v, k_cache, v_cache, out):
             nc.vector.memset(ssum[:, 4:5], 1.0)
             sums.append(ssum)
         ezs = []
-        for i in range(4):
+        for i in range(HK * NJ):
             ez = const.tile([P, S], BF16, name="ez%d" % i)
-            nc.vector.memset(ez[:, HALF - DIAG : HALF], 0.0)
-            nc.vector.memset(ez[:, S - DIAG : S], 0.0)
+            w = HALF - (NJ - 1 - i % NJ) * DIAG
+            if w < HALF:
+                nc.vector.memset(ez[:].rearrange("p (u x) -> p u x", u=2)[:, :, w:HALF], 0.0)
             ezs.append(ez)
         warm = const.tile([P, 1], F32, name="warm")
         nc.vector.memset(warm[:], 0.0)
@@ -129,14 +140,16 @@ def tile_radixattention_t_kernel(tc, q, k, v, k_cache, v_cache, out):
             qt_t[b] = qt
             tp = pool.tile([P, S], BF16, tag=tag)
 
-            def one(i):
+            cols = tp[:].rearrange("p (hk qb jj hh r) -> p hk qb hh jj r", hk=HK, qb=2, jj=2, hh=G)
+
+            def one(qb, h):
                 return lambda: nc.tensor.transpose(
-                    out=tp[:, i * P : (i + 1) * P],
-                    in_=qraw_t[b][:, i // 4, (i % 4) * D : (i % 4 + 1) * D],
+                    out=cols[:, h // G, qb, h % G, :, :],
+                    in_=qraw_t[b][:, qb, h * D : (h + 1) * D],
                     identity=ident[:],
                 )
 
-            return [one(i) for i in range(8)], lambda: copy_out(
+            return [one(qb, h) for qb in range(2) for h in range(H)], lambda: copy_out(
                 on_vector, qt[:].bitcast(F32), tp[:].bitcast(F32)
             )
 
@@ -170,25 +183,25 @@ def tile_radixattention_t_kernel(tc, q, k, v, k_cache, v_cache, out):
             return u // 8, (u % 8) // 4, u % 4
 
         def width(u):
-            return HALF - DIAG if unit(u)[1] == 0 else HALF
+            return HALF - (NJ - 1 - u % NJ) * DIAG
 
         def stage_s(u, half):
-            b, qb, h = unit(u)
+            b, hk, j = unit(u)
             s = ps_s.tile([P, HALF], F32, tag="s")
             w = width(u)
-            lhsT = qt_t[b][:, (qb * 4 + h) * P : (qb * 4 + h + 1) * P]
+            lhsT = qt_t[b][:, (u % 8) * P : (u % 8 + 1) * P]
             c0 = half * HALF
             nc.tensor.matmul(
                 out=s[:, 0 : w - DIAG],
                 lhsT=lhsT,
-                rhs=kt_t[b][:, h // 2, c0 : c0 + w - DIAG],
+                rhs=kt_t[b][:, hk, c0 : c0 + w - DIAG],
                 start=True,
                 stop=True,
             )
             nc.tensor.matmul(
                 out=s[:, w - DIAG : w],
                 lhsT=lhsT,
-                rhs=kt_t[b][:, h // 2, c0 + w - DIAG : c0 + w],
+                rhs=kt_t[b][:, hk, c0 + w - DIAG : c0 + w],
                 start=True,
                 stop=False,
             )
@@ -216,14 +229,11 @@ def tile_radixattention_t_kernel(tc, q, k, v, k_cache, v_cache, out):
             d["m"] = m
 
         def stage_e(u):
-            b, qb, h = unit(u)
             d = st[u]
-            if h == 0:
+            j = u % 4
+            if j == 0:
                 gr[u // 4] = {"ssum": sums[(u // 4) % 6]}
-            if qb == 0:
-                e = ezs[h]
-            else:
-                e = work.tile([P, S], BF16, tag="e")
+            e = ezs[u % 8]
             w = width(u)
             nc.scalar.activation(
                 out=e[:].rearrange("p (u x) -> p u x", u=2)[:, :, 0:w],
@@ -231,7 +241,7 @@ def tile_radixattention_t_kernel(tc, q, k, v, k_cache, v_cache, out):
                 func=ACTF.Exp,
                 bias=d["m"][:],
                 scale=-1.0,
-                accum_out=gr[u // 4]["ssum"][:, h : h + 1],
+                accum_out=gr[u // 4]["ssum"][:, j : j + 1],
             )
             d["e"] = e
 
@@ -263,29 +273,29 @@ def tile_radixattention_t_kernel(tc, q, k, v, k_cache, v_cache, out):
 
         def stage_q(u):
             d = gr[u // 4]
-            h = u % 4
-            if h == 0:
+            j = u % 4
+            if j == 0:
                 ecod = two_buf.tile([P, 8 * P], U32, tag="ecod", align_bytes=64)
                 esc = two_buf.tile([P, 8 * P], U8, tag="esc", align_bytes=64)
                 d["ecod"], d["esc"] = ecod, esc
-            cols = slice(h * 2 * P, (h + 2) * 2 * P)
+            cols = slice(j * 2 * P, (j + 2) * 2 * P)
             nc.vector.quantize_mx(
                 out=d["ecod"][:, cols].bitcast(FP8X4),
                 scales=d["esc"][:, cols],
-                in_=d["gq%d" % h][:].rearrange("p u x -> p (u x)"),
+                in_=d["gq%d" % j][:].rearrange("p u x -> p (u x)"),
             )
 
         def stage_x(su):
-            b = su // 2
+            b, hk = su // 2, su % 2
             d = gr[su]
-            o_ps = ps_o.tile([P, H * D], F32, tag="o")
+            o_ps = ps_o.tile([P, NJ * D], F32, tag="o")
             d["o_ps"] = o_ps
-            for h in range(H):
+            for j in range(NJ):
                 for g in range(2):
-                    vcols = slice((g * HK + h // 2) * D, (g * HK + h // 2 + 1) * D)
-                    ecols = slice((h * 2 + g) * P, (h * 2 + g + 1) * P)
+                    vcols = slice((g * HK + hk) * D, (g * HK + hk + 1) * D)
+                    ecols = slice((j * 2 + g) * P, (j * 2 + g + 1) * P)
                     nc.tensor.matmul_mx(
-                        out=o_ps[:, h * D : (h + 1) * D],
+                        out=o_ps[:, j * D : (j + 1) * D],
                         lhsT=d["ecod"][:, ecols].bitcast(FP8X4),
                         lhsT_scale=d["esc"][:, ecols],
                         rhs=vcod_t[b][:, vcols].bitcast(FP8X4),
@@ -300,16 +310,16 @@ def tile_radixattention_t_kernel(tc, q, k, v, k_cache, v_cache, out):
             gr[su]["rinv"] = rinv
 
         def stage_n(su):
-            b, qb = su // 2, su % 2
-            o_sb = work.tile([P, H, D], F32, tag="o_sb")
+            b, hk = su // 2, su % 2
+            o_sb = work.tile([P, NJ, D], F32, tag="o_sb")
             nc.vector.tensor_tensor(
                 out=o_sb[:],
-                in0=gr[su]["o_ps"][:].rearrange("p (h d) -> p h d", h=H),
-                in1=gr[su]["rinv"][:, 0:4].unsqueeze(2).to_broadcast([P, H, D]),
+                in0=gr[su]["o_ps"][:].rearrange("p (j d) -> p j d", j=NJ),
+                in1=gr[su]["rinv"][:, 0:NJ].unsqueeze(2).to_broadcast([P, NJ, D]),
                 op=ALU.mult,
             )
-            r0 = b * E + qb * P
-            nc.sync.dma_start(out=out[r0 : r0 + P, :], in_=o_sb[:].rearrange("p h d -> p (h d)"))
+            for hh in range(G):
+                nc.sync.dma_start(out=out_v[b, hk, hh], in_=o_sb[hh * R : (hh + 1) * R, :, :])
 
         def run(calls):
             for call in calls:
@@ -344,7 +354,7 @@ def tile_radixattention_t_kernel(tc, q, k, v, k_cache, v_cache, out):
                 tr = stage_t(step - 2)
             if prepare and i in (0, 2, 4):
                 if i == 0:
-                    group = prep_k(nxt, 0, True)
+                    group = prep_k(nxt, 0, nxt % 2 == 1)
                 elif i == 2:
                     group = prep_q(nxt, False)
                 else:

@@ -372,21 +372,21 @@ def tile_radixattention_t_kernel(tc, q, k, v, k_cache, v_cache, out):
                 stage_x((step - 7) // 4)
             if ok(step - 4) and step % 2 == 0:
                 stage_q(step - 4)
+            if ok(step - 6) and (step - 6) % 4 == 0:
+                su = (step - 6) // 4
+                stage_r(su)
+                if step < NU:
+                    one = gr[su]["rinv"][:, NJ : NJ + 1]
+                    if i == 6 and step // 8 + 1 < B:
+                        prep_v_copy(step // 8 + 1, 0, one)
+                    if i == 2 and step >= 8:
+                        prep_v_copy(step // 8, 1, one)
             if ok(step - 2):
                 stage_c(step - 2)
             if step in (-3, -2):
                 prep_v_copy(0, step + 3, 1.0)
             if 0 <= step < NU and i == 5:
                 prep_v_quantize(step // 8)
-            if ok(step - 7) and (step - 7) % 4 == 0:
-                su = (step - 7) // 4
-                stage_r(su)
-                if step < NU:
-                    one = gr[su]["rinv"][:, 4:5]
-                    if i == 7 and step // 8 + 1 < B:
-                        prep_v_copy(step // 8 + 1, 0, one)
-                    if i == 3 and step >= 8:
-                        prep_v_copy(step // 8, 1, one)
             if late:
                 group[1]()
             if prepare and i == 0 and nxt + 2 < B:

@@ -23,6 +23,7 @@ G = H // HK
 NJ = 4
 R = E // NJ
 NU = B * HK * NJ
+LAST = NU // NJ - 1
 HALF = S // 2
 DIAG = R // 2
 
@@ -52,25 +53,41 @@ def tile_radixattention_t_kernel(tc, q, k, v, k_cache, v_cache, out):
         kraw_t, qraw_t, vraw_t = {}, {}, {}
         kt_t, qt_t, vg_t, vcod_t, vsc_t = {}, {}, {}, {}, {}
 
-        def load(b):
+        def load_kq(b):
             qraw = raw.tile([P, 2, H * D], BF16, tag="qraw")
-            nc.sync.dma_start(out=qraw[:], in_=q_v[b])
             kraw = raw.tile([P, 8, HK * D], BF16, tag="kraw")
-            nc.sync.dma_start(out=kraw[:, 0:6, :], in_=kc_v[b])
-            nc.sync.dma_start(out=kraw[:, 6:8, :], in_=k_v[b])
+            if b == 0:
+                nc.sync.dma_start(out=kraw[:, 0:4, :], in_=kc_v[b][:, 0:4, :])
+                nc.scalar.dma_start(out=qraw[:, 0, :], in_=q_v[b][:, 0, :])
+                nc.sync.dma_start(out=kraw[:, 4:6, :], in_=kc_v[b][:, 4:6, :])
+                nc.sync.dma_start(out=kraw[:, 6:8, :], in_=k_v[b])
+                nc.scalar.dma_start(out=qraw[:, 1, :], in_=q_v[b][:, 1, :])
+            else:
+                nc.sync.dma_start(out=kraw[:, 0:6, :], in_=kc_v[b])
+                nc.sync.dma_start(out=kraw[:, 6:8, :], in_=k_v[b])
+                nc.sync.dma_start(out=qraw[:], in_=q_v[b])
+            kraw_t[b], qraw_t[b] = kraw, qraw
+
+        def load_v(b):
             vraw = raw.tile([P, 2, 4, HK * D], BF16, tag="vraw")
             nc.sync.dma_start(out=vraw[:, 0, :, :], in_=vc_v[b, 0:P])
             nc.sync.dma_start(out=vraw[0:64, 1, :, :], in_=vc_v[b, P : P + 64])
             nc.sync.dma_start(out=vraw[64:P, 1, :, :], in_=v_v[b])
-            kraw_t[b], qraw_t[b], vraw_t[b] = kraw, qraw, vraw
+            vraw_t[b] = vraw
 
-        for b in range(3):
-            load(b)
+        for b in range(2):
+            load_kq(b)
+        for b in range(2):
+            load_v(b)
+        load_kq(2)
+        load_v(2)
 
+        warm = const.tile([P, 1], F32, name="warm")
+        nc.vector.memset(warm[:], 0.0)
+        warm2 = const.tile([P, 1], F32, name="warm2")
+        nc.scalar.activation(out=warm2[:], in_=warm[:], func=ACTF.Exp)
         ident = const.tile([P, P], BF16, name="ident")
         make_identity(nc, ident[:])
-        ident32 = const.tile([P, P], F32, name="ident32")
-        make_identity(nc, ident32[:])
         mask_h = []
         for hh in range(G):
             mh = const.tile([P, R], F32, name="mask_h%d" % hh)
@@ -86,6 +103,8 @@ def tile_radixattention_t_kernel(tc, q, k, v, k_cache, v_cache, out):
             )
             mask_h.append(mh)
         nc.gpsimd.memset(mask_h[1][0:R, :], 0.0)
+        ident32 = const.tile([P, P], F32, name="ident32")
+        make_identity(nc, ident32[:])
         mask = const.tile([P, 2, DIAG], BF16, name="mask")
         nc.vector.tensor_tensor(
             out=mask[:].rearrange("p u (z e) -> p u z e", e=2),
@@ -105,52 +124,51 @@ def tile_radixattention_t_kernel(tc, q, k, v, k_cache, v_cache, out):
             if w < HALF:
                 nc.vector.memset(ez[:].rearrange("p (u x) -> p u x", u=2)[:, :, w:HALF], 0.0)
             ezs.append(ez)
-        warm = const.tile([P, 1], F32, name="warm")
-        nc.vector.memset(warm[:], 0.0)
-        warm2 = const.tile([P, 1], F32, name="warm2")
-        nc.scalar.activation(out=warm2[:], in_=warm[:], func=ACTF.Exp)
-
         def copy_out(on_vector, dst, src):
             if on_vector:
                 nc.vector.tensor_copy(out=dst, in_=src)
             else:
                 nc.scalar.copy(out=dst, in_=src)
 
-        def prep_k(b, hk, on_vector, pool=ps_p, tag="p"):
-            if hk == 0:
+        def prep_k(b, hk, on_vector, pool=ps_p, tag="p", g0=0, g1=2):
+            if b not in kt_t:
                 kt = prep.tile([P, HK, S], BF16, tag="kt")
                 kt_t[b] = kt
             tp = pool.tile([P, S], BF16, tag=tag)
+            n = (g1 - g0) * 4
 
             def one(c):
                 return lambda: nc.tensor.transpose(
                     out=tp[:, c * P : (c + 1) * P],
-                    in_=kraw_t[b][:, c, hk * D : (hk + 1) * D],
+                    in_=kraw_t[b][:, 4 * g0 + c, hk * D : (hk + 1) * D],
                     identity=ident[:],
                 )
 
-            return [one(c) for c in range(8)], lambda: copy_out(
+            return [one(c) for c in range(n)], lambda: copy_out(
                 on_vector,
-                kt_t[b][:, hk, :].bitcast(F32).rearrange("p (u x) -> p u x", u=2),
-                tp[:].bitcast(F32).rearrange("p (x u) -> p u x", u=2),
+                kt_t[b][:, hk, :].bitcast(F32).rearrange("p (u x) -> p u x", u=2)[:, :, g0 * P : g1 * P],
+                tp[:, 0 : n * P].bitcast(F32).rearrange("p (x u) -> p u x", u=2),
             )
 
-        def prep_q(b, on_vector, pool=ps_p, tag="p"):
-            qt = prep.tile([P, 8 * P], BF16, tag="qt")
-            qt_t[b] = qt
+        def prep_q(b, on_vector, pool=ps_p, tag="p", i0=0, i1=4):
+            if b not in qt_t:
+                qt = prep.tile([P, 8 * P], BF16, tag="qt")
+                qt_t[b] = qt
             tp = pool.tile([P, S], BF16, tag=tag)
 
             cols = tp[:].rearrange("p (hk qb jj hh r) -> p hk qb hh jj r", hk=HK, qb=2, jj=2, hh=G)
 
-            def one(qb, h):
+            def one(hk, qb, hh):
+                h = hk * G + hh
                 return lambda: nc.tensor.transpose(
-                    out=cols[:, h // G, qb, h % G, :, :],
+                    out=cols[:, hk, qb, hh, :, :],
                     in_=qraw_t[b][:, qb, h * D : (h + 1) * D],
                     identity=ident[:],
                 )
 
-            return [one(qb, h) for qb in range(2) for h in range(H)], lambda: copy_out(
-                on_vector, qt[:].bitcast(F32), tp[:].bitcast(F32)
+            used = slice(i0 * 2 * P, i1 * 2 * P)
+            return [one(i // 2, i % 2, hh) for i in range(i0, i1) for hh in range(G)], lambda: copy_out(
+                on_vector, qt_t[b][:, used].bitcast(F32), tp[:, used].bitcast(F32)
             )
 
         def prep_v_copy(b, g, one):
@@ -249,12 +267,17 @@ def tile_radixattention_t_kernel(tc, q, k, v, k_cache, v_cache, out):
             d = st[u]
             tp = ps_t.tile([P, 2, 2, P], F32, tag="t")
             d["tp"] = tp
+            banks = (tp, tp)
+            if u == NU - 1:
+                tp_b = ps_s.tile([P, 2, 2, P], F32, tag="s")
+                d["tp_b"] = tp_b
+                banks = (tp, tp_b)
             words = d["e"][:].bitcast(F32)
 
             def one(g, half):
                 w0 = half * (HALF // 2) + g * P
                 return lambda: nc.tensor.transpose(
-                    out=tp[:, g, half, :], in_=words[:, w0 : w0 + P], identity=ident32[:]
+                    out=banks[g][:, g, half, :], in_=words[:, w0 : w0 + P], identity=ident32[:]
                 )
 
             return [one(g, half) for g in range(2) for half in range(2)]
@@ -266,31 +289,32 @@ def tile_radixattention_t_kernel(tc, q, k, v, k_cache, v_cache, out):
                 gr[u // 4]["gq%d" % (u % 4)] = gq
             else:
                 gq = gr[u // 4]["gq%d" % (u % 4 - 1)]
-            nc.scalar.copy(
-                out=gq[:, u % 2, :].bitcast(F32).rearrange("p (g r u) -> p g r u", g=2, u=2),
-                in_=d["tp"][:].rearrange("p g u r -> p g r u"),
-            )
+            words = gq[:, u % 2, :].bitcast(F32).rearrange("p (g r u) -> p g r u", g=2, u=2)
+            if u == NU - 1:
+                copy_out(True, words[:, 0], d["tp"][:, 0].rearrange("p u r -> p r u"))
+                copy_out(False, words[:, 1], d["tp_b"][:, 1].rearrange("p u r -> p r u"))
+            else:
+                copy_out(u >= NU - 3, words, d["tp"][:].rearrange("p g u r -> p g r u"))
 
-        def stage_q(u):
+        def stage_q(u, n=2):
             d = gr[u // 4]
             j = u % 4
             if j == 0:
                 ecod = two_buf.tile([P, 8 * P], U32, tag="ecod", align_bytes=64)
                 esc = two_buf.tile([P, 8 * P], U8, tag="esc", align_bytes=64)
                 d["ecod"], d["esc"] = ecod, esc
-            cols = slice(j * 2 * P, (j + 2) * 2 * P)
+            cols = slice(j * 2 * P, (j + n) * 2 * P)
+            gq = d["gq%d" % (j - j % 2)]
             nc.vector.quantize_mx(
                 out=d["ecod"][:, cols].bitcast(FP8X4),
                 scales=d["esc"][:, cols],
-                in_=d["gq%d" % j][:].rearrange("p u x -> p (u x)"),
+                in_=gq[:, j % 2 : j % 2 + n, :].rearrange("p u x -> p (u x)"),
             )
 
-        def stage_x(su):
+        def stage_x(su, o_ps, j0=0, j1=NJ):
             b, hk = su // 2, su % 2
             d = gr[su]
-            o_ps = ps_o.tile([P, NJ * D], F32, tag="o")
-            d["o_ps"] = o_ps
-            for j in range(NJ):
+            for j in range(j0, j1):
                 for g in range(2):
                     vcols = slice((g * HK + hk) * D, (g * HK + hk + 1) * D)
                     ecols = slice((j * 2 + g) * P, (j * 2 + g + 1) * P)
@@ -309,17 +333,20 @@ def tile_radixattention_t_kernel(tc, q, k, v, k_cache, v_cache, out):
             nc.vector.reciprocal(out=rinv[:], in_=gr[su]["ssum"][:])
             gr[su]["rinv"] = rinv
 
-        def stage_n(su):
+        def stage_n(su, o_ps, j0=0, j1=NJ):
             b, hk = su // 2, su % 2
+            n = j1 - j0
             o_sb = work.tile([P, NJ, D], F32, tag="o_sb")
             nc.vector.tensor_tensor(
-                out=o_sb[:],
-                in0=gr[su]["o_ps"][:].rearrange("p (j d) -> p j d", j=NJ),
-                in1=gr[su]["rinv"][:, 0:NJ].unsqueeze(2).to_broadcast([P, NJ, D]),
+                out=o_sb[:, j0:j1, :],
+                in0=o_ps[:, j0 * D : j1 * D].rearrange("p (j d) -> p j d", j=n),
+                in1=gr[su]["rinv"][:, j0:j1].unsqueeze(2).to_broadcast([P, n, D]),
                 op=ALU.mult,
             )
             for hh in range(G):
-                nc.sync.dma_start(out=out_v[b, hk, hh], in_=o_sb[hh * R : (hh + 1) * R, :, :])
+                nc.sync.dma_start(
+                    out=out_v[b, hk, hh][:, j0:j1, :], in_=o_sb[hh * R : (hh + 1) * R, j0:j1, :]
+                )
 
         def run(calls):
             for call in calls:
@@ -328,25 +355,36 @@ def tile_radixattention_t_kernel(tc, q, k, v, k_cache, v_cache, out):
         def ok(u):
             return 0 <= u < NU
 
-        first = prep_q(0, False, ps_t, "t")
-        run(first[0])
-        first[1]()
-        first = prep_k(0, 0, True, ps_t, "t")
-        run(first[0])
-        first[1]()
-        group = prep_k(0, 1, False)
-        waiting = group[0]
+        k00 = prep_k(0, 0, True, ps_t, "t", 0, 1)
+        q00 = prep_q(0, False, i1=1)
+        k01 = prep_k(0, 0, False, ps_t, "t", 1, 2)
+        k1 = prep_k(0, 1, False, ps_o, "o")
+        for part in (k00, q00, k01, k1):
+            run(part[0])
+            part[1]()
+        stage_s(0, 0)
+        stage_s(0, 1)
+        q_rest = prep_q(0, False, i0=1)
+        run(q_rest[0])
+        q_rest[1]()
+        stage_m(0, 0)
+        stage_m(0, 1)
+        stage_s(1, 0)
+        stage_s(1, 1)
+        stage_m(1, 0)
+        stage_s(2, 0)
+        waiting = []
 
-        for step in range(-3, NU + 9):
+        for step in range(NU + 2):
             nxt = step // 8 + 1
             i = step % 8
-            prepare = 0 <= step < NU and nxt < B
+            prepare = nxt < B
             if ok(step - 1):
                 stage_e(step - 1)
             if ok(step + 2):
                 stage_m(step + 2, 0)
             if ok(step - 8) and (step - 8) % 4 == 0:
-                stage_n((step - 8) // 4)
+                stage_n((step - 8) // 4, o_ps)
             if ok(step + 1):
                 stage_m(step + 1, 1)
             tr = []
@@ -369,7 +407,8 @@ def tile_radixattention_t_kernel(tc, q, k, v, k_cache, v_cache, out):
             if ok(step + 2):
                 stage_s(step + 2, 1)
             if ok(step - 7) and (step - 7) % 4 == 0:
-                stage_x((step - 7) // 4)
+                o_ps = ps_o.tile([P, NJ * D], F32, tag="o")
+                stage_x((step - 7) // 4, o_ps)
             if ok(step - 4) and step % 2 == 0:
                 stage_q(step - 4)
             if ok(step - 6) and (step - 6) % 4 == 0:
@@ -381,13 +420,27 @@ def tile_radixattention_t_kernel(tc, q, k, v, k_cache, v_cache, out):
                         prep_v_copy(step // 8 + 1, 0, one)
                     if i == 2 and step >= 8:
                         prep_v_copy(step // 8, 1, one)
+            if step == NU:
+                o_01 = ps_o.tile([P, NJ * D], F32, tag="o")
+                stage_x(LAST, o_01, 0, 2)
+            if step == NU + 1:
+                o_23 = ps_p.tile([P, NJ * D], F32, tag="p")
+                stage_q(NU - 2, 1)
+                stage_x(LAST, o_23, 2, 3)
+                stage_r(LAST)
+                stage_n(LAST, o_01, 0, 2)
             if ok(step - 2):
                 stage_c(step - 2)
-            if step in (-3, -2):
-                prep_v_copy(0, step + 3, 1.0)
-            if 0 <= step < NU and i == 5:
+            if step == NU + 1:
+                stage_q(NU - 1, 1)
+                stage_x(LAST, o_23, 3, 4)
+                stage_n(LAST, o_23, 2, 4)
+            if step < 2:
+                prep_v_copy(0, step, 1.0)
+            if step < NU and i == 5:
                 prep_v_quantize(step // 8)
             if late:
                 group[1]()
             if prepare and i == 0 and nxt + 2 < B:
-                load(nxt + 2)
+                load_kq(nxt + 2)
+                load_v(nxt + 2)

@@ -26,6 +26,7 @@ NU = B * HK * NJ
 LAST = NU // NJ - 1
 HALF = S // 2
 DIAG = R // 2
+WIDE = 96
 
 
 def tile_radixattention_t_kernel(tc, q, k, v, k_cache, v_cache, out):
@@ -35,7 +36,7 @@ def tile_radixattention_t_kernel(tc, q, k, v, k_cache, v_cache, out):
         const = ctx.enter_context(tc.tile_pool(name="const", bufs=1))
         raw = ctx.enter_context(tc.tile_pool(name="raw", bufs=4))
         prep = ctx.enter_context(tc.tile_pool(name="prep", bufs=2))
-        work = ctx.enter_context(tc.tile_pool(name="work", bufs=4))
+        work = ctx.enter_context(tc.tile_pool(name="work", bufs=6))
         two_buf = ctx.enter_context(tc.tile_pool(name="two_buf", bufs=2))
         small = ctx.enter_context(tc.tile_pool(name="small", bufs=6))
         ps_s = ctx.enter_context(tc.psum_pool(name="ps_s", bufs=4))
@@ -105,9 +106,10 @@ def tile_radixattention_t_kernel(tc, q, k, v, k_cache, v_cache, out):
         nc.gpsimd.memset(mask_h[1][0:R, :], 0.0)
         ident32 = const.tile([P, P], F32, name="ident32")
         make_identity(nc, ident32[:])
-        mask = const.tile([P, 2, DIAG], BF16, name="mask")
+        mask = const.tile([P, 2, WIDE], BF16, name="mask")
+        nc.vector.memset(mask[:], 0.0)
         nc.vector.tensor_tensor(
-            out=mask[:].rearrange("p u (z e) -> p u z e", e=2),
+            out=mask[:, :, WIDE - DIAG : WIDE].rearrange("p u (z e) -> p u z e", e=2),
             in0=mask_h[0][:].rearrange("p (z u e) -> p u z e", u=2, e=2),
             in1=mask_h[1][:].rearrange("p (z u e) -> p u z e", u=2, e=2),
             op=ALU.add,
@@ -210,21 +212,10 @@ def tile_radixattention_t_kernel(tc, q, k, v, k_cache, v_cache, out):
             lhsT = qt_t[b][:, (u % 8) * P : (u % 8 + 1) * P]
             c0 = half * HALF
             nc.tensor.matmul(
-                out=s[:, 0 : w - DIAG],
-                lhsT=lhsT,
-                rhs=kt_t[b][:, hk, c0 : c0 + w - DIAG],
-                start=True,
-                stop=True,
+                out=s[:, 0:w], lhsT=lhsT, rhs=kt_t[b][:, hk, c0 : c0 + w], start=True, stop=False
             )
             nc.tensor.matmul(
-                out=s[:, w - DIAG : w],
-                lhsT=lhsT,
-                rhs=kt_t[b][:, hk, c0 + w - DIAG : c0 + w],
-                start=True,
-                stop=False,
-            )
-            nc.tensor.matmul(
-                out=s[:, w - DIAG : w], lhsT=ident[:], rhs=mask[:, half, :], start=False, stop=True
+                out=s[:, w - WIDE : w], lhsT=ident[:], rhs=mask[:, half, :], start=False, stop=True
             )
             st.setdefault(u, {})[half] = s
 
@@ -401,9 +392,9 @@ def tile_radixattention_t_kernel(tc, q, k, v, k_cache, v_cache, out):
             late = 0 < len(waiting) <= 4
             tr = tr + waiting[0:4]
             waiting = waiting[4:]
+            run(tr)
             if ok(step + 3):
                 stage_s(step + 3, 0)
-            run(tr)
             if ok(step + 2):
                 stage_s(step + 2, 1)
             if ok(step - 7) and (step - 7) % 4 == 0:

from contextlib import ExitStack
import math

import concourse.mybir as mybir
from concourse.masks import make_identity

FP8X4 = mybir.dt.float8_e4m3fn_x4
BF16 = mybir.dt.bfloat16
F32 = mybir.dt.float32
U32 = mybir.dt.uint32
U8 = mybir.dt.uint8
ALU = mybir.AluOpType
ACTF = mybir.ActivationFunctionType

B, E, PRE, H, HK, D = 16, 256, 768, 4, 2, 128
S = PRE + E
P = 128
SCALING = 1.0 / math.sqrt(D)
NEG = -1.0e30
FLOPS = 2 * 2 * B * H * E * S * D

G = H // HK
NJ = 4
R = E // NJ
NU = B * HK * NJ
LAST = NU // NJ - 1
HALF = S // 2
DIAG = R // 2
WIDE = 96


def tile_radixattention_t_kernel(tc, q, k, v, k_cache, v_cache, out):
    nc = tc.nc
    with ExitStack() as ctx:
        ctx.enter_context(tc.manual_schedule())
        const = ctx.enter_context(tc.tile_pool(name="const", bufs=1))
        raw = ctx.enter_context(tc.tile_pool(name="raw", bufs=4))
        prep = ctx.enter_context(tc.tile_pool(name="prep", bufs=2))
        work = ctx.enter_context(tc.tile_pool(name="work", bufs=6))
        two_buf = ctx.enter_context(tc.tile_pool(name="two_buf", bufs=2))
        small = ctx.enter_context(tc.tile_pool(name="small", bufs=6))
        ps_s = ctx.enter_context(tc.psum_pool(name="ps_s", bufs=4))
        ps_t = ctx.enter_context(tc.psum_pool(name="ps_t", bufs=2))
        ps_p = ctx.enter_context(tc.psum_pool(name="ps_p", bufs=1))
        ps_o = ctx.enter_context(tc.psum_pool(name="ps_o", bufs=1))

        q_v = q.rearrange("b (qb p) h d -> b p qb (h d)", p=P)
        k_v = k.rearrange("b (c p) hk d -> b p c (hk d)", p=P)
        kc_v = k_cache.rearrange("b (c p) hk d -> b p c (hk d)", p=P)
        out_v = out.rearrange("(b j r) (hk hh d) -> b hk hh r j d", j=NJ, r=R, hk=HK, hh=G)
        v_v = v.rearrange("b (p t) hk d -> b p t (hk d)", t=4)
        vc_v = v_cache.rearrange("b (gp t) hk d -> b gp t (hk d)", t=4)

        kraw_t, qraw_t, vraw_t = {}, {}, {}
        kt_t, qt_t, vg_t, vcod_t, vsc_t = {}, {}, {}, {}, {}

        def load_kq(b):
            qraw = raw.tile([P, 2, H * D], BF16, tag="qraw")
            kraw = raw.tile([P, 8, HK * D], BF16, tag="kraw")
            if b == 0:
                nc.sync.dma_start(out=kraw[:, 0:4, :], in_=kc_v[b][:, 0:4, :])
                nc.scalar.dma_start(out=qraw[:, 0, :], in_=q_v[b][:, 0, :])
                nc.sync.dma_start(out=kraw[:, 4:6, :], in_=kc_v[b][:, 4:6, :])
                nc.sync.dma_start(out=kraw[:, 6:8, :], in_=k_v[b])
                nc.scalar.dma_start(out=qraw[:, 1, :], in_=q_v[b][:, 1, :])
            else:
                nc.sync.dma_start(out=kraw[:, 0:6, :], in_=kc_v[b])
                nc.sync.dma_start(out=kraw[:, 6:8, :], in_=k_v[b])
                nc.sync.dma_start(out=qraw[:], in_=q_v[b])
            kraw_t[b], qraw_t[b] = kraw, qraw

        def load_v(b):
            vraw = raw.tile([P, 2, 4, HK * D], BF16, tag="vraw")
            nc.sync.dma_start(out=vraw[:, 0, :, :], in_=vc_v[b, 0:P])
            nc.sync.dma_start(out=vraw[0:64, 1, :, :], in_=vc_v[b, P : P + 64])
            nc.sync.dma_start(out=vraw[64:P, 1, :, :], in_=v_v[b])
            vraw_t[b] = vraw

        for b in range(2):
            load_kq(b)
        for b in range(2):
            load_v(b)
        load_kq(2)
        load_v(2)

        warm = const.tile([P, 1], F32, name="warm")
        nc.vector.memset(warm[:], 0.0)
        warm2 = const.tile([P, 1], F32, name="warm2")
        nc.scalar.activation(out=warm2[:], in_=warm[:], func=ACTF.Exp)
        ident = const.tile([P, P], BF16, name="ident")
        make_identity(nc, ident[:])
        mask_h = []
        for hh in range(G):
            mh = const.tile([P, R], F32, name="mask_h%d" % hh)
            nc.gpsimd.memset(mh[:], 0.0)
            nc.gpsimd.affine_select(
                out=mh[:],
                in_=mh[:],
                compare_op=ALU.is_ge,
                fill=NEG,
                base=-hh * R,
                pattern=[[-1, R]],
                channel_multiplier=1,
            )
            mask_h.append(mh)
        nc.gpsimd.memset(mask_h[1][0:R, :], 0.0)
        ident32 = const.tile([P, P], F32, name="ident32")
        make_identity(nc, ident32[:])
        mask = const.tile([P, 2, WIDE], BF16, name="mask")
        nc.vector.memset(mask[:], 0.0)
        nc.vector.tensor_tensor(
            out=mask[:, :, WIDE - DIAG : WIDE].rearrange("p u (z e) -> p u z e", e=2),
            in0=mask_h[0][:].rearrange("p (z u e) -> p u z e", u=2, e=2),
            in1=mask_h[1][:].rearrange("p (z u e) -> p u z e", u=2, e=2),
            op=ALU.add,
        )
        sums = []
        for i in range(6):
            ssum = const.tile([P, 5], F32, name="ssum%d" % i)
            nc.vector.memset(ssum[:, 4:5], 1.0)
            sums.append(ssum)
        ezs = []
        for i in range(HK * NJ):
            ez = const.tile([P, S], BF16, name="ez%d" % i)
            w = HALF - (NJ - 1 - i % NJ) * DIAG
            if w < HALF:
                nc.vector.memset(ez[:].rearrange("p (u x) -> p u x", u=2)[:, :, w:HALF], 0.0)
            ezs.append(ez)
        def copy_out(on_vector, dst, src):
            if on_vector:
                nc.vector.tensor_copy(out=dst, in_=src)
            else:
                nc.scalar.copy(out=dst, in_=src)

        def prep_k(b, hk, on_vector, pool=ps_p, tag="p", g0=0, g1=2):
            if b not in kt_t:
                kt = prep.tile([P, HK, S], BF16, tag="kt")
                kt_t[b] = kt
            tp = pool.tile([P, S], BF16, tag=tag)
            n = (g1 - g0) * 4

            def one(c):
                return lambda: nc.tensor.transpose(
                    out=tp[:, c * P : (c + 1) * P],
                    in_=kraw_t[b][:, 4 * g0 + c, hk * D : (hk + 1) * D],
                    identity=ident[:],
                )

            return [one(c) for c in range(n)], lambda: copy_out(
                on_vector,
                kt_t[b][:, hk, :].bitcast(F32).rearrange("p (u x) -> p u x", u=2)[:, :, g0 * P : g1 * P],
                tp[:, 0 : n * P].bitcast(F32).rearrange("p (x u) -> p u x", u=2),
            )

        def prep_q(b, on_vector, pool=ps_p, tag="p", i0=0, i1=4):
            if b not in qt_t:
                qt = prep.tile([P, 8 * P], BF16, tag="qt")
                qt_t[b] = qt
            tp = pool.tile([P, S], BF16, tag=tag)

            cols = tp[:].rearrange("p (hk qb jj hh r) -> p hk qb hh jj r", hk=HK, qb=2, jj=2, hh=G)

            def one(hk, qb, hh):
                h = hk * G + hh
                return lambda: nc.tensor.transpose(
                    out=cols[:, hk, qb, hh, :, :],
                    in_=qraw_t[b][:, qb, h * D : (h + 1) * D],
                    identity=ident[:],
                )

            used = slice(i0 * 2 * P, i1 * 2 * P)
            return [one(i // 2, i % 2, hh) for i in range(i0, i1) for hh in range(G)], lambda: copy_out(
                on_vector, qt_t[b][:, used].bitcast(F32), tp[:, used].bitcast(F32)
            )

        def prep_v_copy(b, g, one):
            if g == 0:
                vg = prep.tile([P, 2, HK * D, 4], BF16, tag="vg", align_bytes=64)
                vg_t[b] = vg
            nc.gpsimd.tensor_scalar(
                out=vg_t[b][:, g, :, :],
                in0=vraw_t[b][:, g, :, :].rearrange("p t x -> p x t"),
                scalar1=one,
                scalar2=0.0,
                op0=ALU.mult,
                op1=ALU.add,
            )

        def prep_v_quantize(b):
            vcod = prep.tile([P, 2 * HK * D], U32, tag="vcod", align_bytes=64)
            vsc = prep.tile([P, 2 * HK * D], U8, tag="vsc", align_bytes=64)
            vcod_t[b], vsc_t[b] = vcod, vsc
            nc.vector.quantize_mx(
                out=vcod[:].bitcast(FP8X4),
                scales=vsc[:],
                in_=vg_t[b][:].rearrange("p g x t -> p (g x t)"),
            )

        st = {}
        gr = {}

        def unit(u):
            return u // 8, (u % 8) // 4, u % 4

        def width(u):
            return HALF - (NJ - 1 - u % NJ) * DIAG

        def stage_s(u, half):
            b, hk, j = unit(u)
            s = ps_s.tile([P, HALF], F32, tag="s")
            w = width(u)
            lhsT = qt_t[b][:, (u % 8) * P : (u % 8 + 1) * P]
            c0 = half * HALF
            nc.tensor.matmul(
                out=s[:, 0:w], lhsT=lhsT, rhs=kt_t[b][:, hk, c0 : c0 + w], start=True, stop=False
            )
            nc.tensor.matmul(
                out=s[:, w - WIDE : w], lhsT=ident[:], rhs=mask[:, half, :], start=False, stop=True
            )
            st.setdefault(u, {})[half] = s

        def stage_m(u, half):
            d = st[u]
            w = width(u)
            if half == 0:
                ssb = work.tile([P, S], F32, tag="ssb")
                d["ssb"] = ssb
            m = small.tile([P, 1], F32, tag="m%d" % half)
            nc.vector.tensor_scalar(
                out=d["ssb"][:, half * HALF : half * HALF + w],
                in0=d[half][:, 0:w],
                scalar1=-SCALING,
                scalar2=None if half == 0 else d["m"][:, 0:1],
                op0=ALU.mult,
                op1=ALU.min,
                accum_out=m[:],
            )
            d["m"] = m

        def stage_e(u):
            d = st[u]
            j = u % 4
            if j == 0:
                gr[u // 4] = {"ssum": sums[(u // 4) % 6]}
            e = ezs[u % 8]
            w = width(u)
            nc.scalar.activation(
                out=e[:].rearrange("p (u x) -> p u x", u=2)[:, :, 0:w],
                in_=d["ssb"][:].rearrange("p (u x) -> p u x", u=2)[:, :, 0:w],
                func=ACTF.Exp,
                bias=d["m"][:],
                scale=-1.0,
                accum_out=gr[u // 4]["ssum"][:, j : j + 1],
            )
            d["e"] = e

        def stage_t(u):
            d = st[u]
            tp = ps_t.tile([P, 2, 2, P], F32, tag="t")
            d["tp"] = tp
            banks = (tp, tp)
            if u == NU - 1:
                tp_b = ps_s.tile([P, 2, 2, P], F32, tag="s")
                d["tp_b"] = tp_b
                banks = (tp, tp_b)
            words = d["e"][:].bitcast(F32)

            def one(g, half):
                w0 = half * (HALF // 2) + g * P
                return lambda: nc.tensor.transpose(
                    out=banks[g][:, g, half, :], in_=words[:, w0 : w0 + P], identity=ident32[:]
                )

            return [one(g, half) for g in range(2) for half in range(2)]

        def stage_c(u):
            d = st[u]
            if u % 2 == 0:
                gq = work.tile([P, 2, S], BF16, tag="gq", align_bytes=64)
                gr[u // 4]["gq%d" % (u % 4)] = gq
            else:
                gq = gr[u // 4]["gq%d" % (u % 4 - 1)]
            words = gq[:, u % 2, :].bitcast(F32).rearrange("p (g r u) -> p g r u", g=2, u=2)
            if u == NU - 1:
                copy_out(True, words[:, 0], d["tp"][:, 0].rearrange("p u r -> p r u"))
                copy_out(False, words[:, 1], d["tp_b"][:, 1].rearrange("p u r -> p r u"))
            else:
                copy_out(u >= NU - 3, words, d["tp"][:].rearrange("p g u r -> p g r u"))

        def stage_q(u, n=2):
            d = gr[u // 4]
            j = u % 4
            if j == 0:
                ecod = two_buf.tile([P, 8 * P], U32, tag="ecod", align_bytes=64)
                esc = two_buf.tile([P, 8 * P], U8, tag="esc", align_bytes=64)
                d["ecod"], d["esc"] = ecod, esc
            cols = slice(j * 2 * P, (j + n) * 2 * P)
            gq = d["gq%d" % (j - j % 2)]
            nc.vector.quantize_mx(
                out=d["ecod"][:, cols].bitcast(FP8X4),
                scales=d["esc"][:, cols],
                in_=gq[:, j % 2 : j % 2 + n, :].rearrange("p u x -> p (u x)"),
            )

        def stage_x(su, o_ps, j0=0, j1=NJ):
            b, hk = su // 2, su % 2
            d = gr[su]
            for j in range(j0, j1):
                for g in range(2):
                    vcols = slice((g * HK + hk) * D, (g * HK + hk + 1) * D)
                    ecols = slice((j * 2 + g) * P, (j * 2 + g + 1) * P)
                    nc.tensor.matmul_mx(
                        out=o_ps[:, j * D : (j + 1) * D],
                        lhsT=d["ecod"][:, ecols].bitcast(FP8X4),
                        lhsT_scale=d["esc"][:, ecols],
                        rhs=vcod_t[b][:, vcols].bitcast(FP8X4),
                        rhs_scale=vsc_t[b][:, vcols],
                        start=(g == 0),
                        stop=(g == 1),
                    )

        def stage_r(su):
            rinv = small.tile([P, 5], F32, tag="rinv")
            nc.vector.reciprocal(out=rinv[:], in_=gr[su]["ssum"][:])
            gr[su]["rinv"] = rinv

        def stage_n(su, o_ps, j0=0, j1=NJ):
            b, hk = su // 2, su % 2
            n = j1 - j0
            o_sb = work.tile([P, NJ, D], F32, tag="o_sb")
            nc.vector.tensor_tensor(
                out=o_sb[:, j0:j1, :],
                in0=o_ps[:, j0 * D : j1 * D].rearrange("p (j d) -> p j d", j=n),
                in1=gr[su]["rinv"][:, j0:j1].unsqueeze(2).to_broadcast([P, n, D]),
                op=ALU.mult,
            )
            for hh in range(G):
                nc.sync.dma_start(
                    out=out_v[b, hk, hh][:, j0:j1, :], in_=o_sb[hh * R : (hh + 1) * R, j0:j1, :]
                )

        def run(calls):
            for call in calls:
                call()

        def ok(u):
            return 0 <= u < NU

        k00 = prep_k(0, 0, True, ps_t, "t", 0, 1)
        q00 = prep_q(0, False, i1=1)
        k01 = prep_k(0, 0, False, ps_t, "t", 1, 2)
        k1 = prep_k(0, 1, False, ps_o, "o")
        for part in (k00, q00, k01, k1):
            run(part[0])
            part[1]()
        stage_s(0, 0)
        stage_s(0, 1)
        q_rest = prep_q(0, False, i0=1)
        run(q_rest[0])
        q_rest[1]()
        stage_m(0, 0)
        stage_m(0, 1)
        stage_s(1, 0)
        stage_s(1, 1)
        stage_m(1, 0)
        stage_s(2, 0)
        waiting = []

        for step in range(NU + 2):
            nxt = step // 8 + 1
            i = step % 8
            prepare = nxt < B
            if ok(step - 1):
                stage_e(step - 1)
            if ok(step + 2):
                stage_m(step + 2, 0)
            if ok(step - 8) and (step - 8) % 4 == 0:
                stage_n((step - 8) // 4, o_ps)
            if ok(step + 1):
                stage_m(step + 1, 1)
            tr = []
            if ok(step - 2):
                tr = stage_t(step - 2)
            if prepare and i in (0, 2, 4):
                if i == 0:
                    group = prep_k(nxt, 0, nxt % 2 == 1)
                elif i == 2:
                    group = prep_q(nxt, False)
                else:
                    group = prep_k(nxt, 1, False)
                waiting = group[0]
            late = 0 < len(waiting) <= 4
            tr = tr + waiting[0:4]
            waiting = waiting[4:]
            run(tr)
            if ok(step + 3):
                stage_s(step + 3, 0)
            if ok(step + 2):
                stage_s(step + 2, 1)
            if ok(step - 7) and (step - 7) % 4 == 0:
                o_ps = ps_o.tile([P, NJ * D], F32, tag="o")
                stage_x((step - 7) // 4, o_ps)
            if ok(step - 4) and step % 2 == 0:
                stage_q(step - 4)
            if ok(step - 6) and (step - 6) % 4 == 0:
                su = (step - 6) // 4
                stage_r(su)
                if step < NU:
                    one = gr[su]["rinv"][:, NJ : NJ + 1]
                    if i == 6 and step // 8 + 1 < B:
                        prep_v_copy(step // 8 + 1, 0, one)
                    if i == 2 and step >= 8:
                        prep_v_copy(step // 8, 1, one)
            if step == NU:
                o_01 = ps_o.tile([P, NJ * D], F32, tag="o")
                stage_x(LAST, o_01, 0, 2)
            if step == NU + 1:
                o_23 = ps_p.tile([P, NJ * D], F32, tag="p")
                stage_q(NU - 2, 1)
                stage_x(LAST, o_23, 2, 3)
                stage_r(LAST)
                stage_n(LAST, o_01, 0, 2)
            if ok(step - 2):
                stage_c(step - 2)
            if step == NU + 1:
                stage_q(NU - 1, 1)
                stage_x(LAST, o_23, 3, 4)
                stage_n(LAST, o_23, 2, 4)
            if step < 2:
                prep_v_copy(0, step, 1.0)
            if step < NU and i == 5:
                prep_v_quantize(step // 8)
            if late:
                group[1]()
            if prepare and i == 0 and nxt + 2 < B:
                load_kq(nxt + 2)
                load_v(nxt + 2)
